import numpy as np
import ml_dtypes


def mxq(x, axis, fmt="e4m3"):
    dtype, down = {"e4m3": (ml_dtypes.float8_e4m3fn, 7), "e5m2": (ml_dtypes.float8_e5m2, 14)}[fmt]
    v = np.moveaxis(np.asarray(x, np.float32).astype(ml_dtypes.bfloat16).astype(np.float64), axis, -1)
    blocks = v.reshape(v.shape[:-1] + (-1, 32))
    amax = np.abs(blocks).max(-1, keepdims=True)
    byte = np.maximum(np.where(amax > 0, np.frexp(amax)[1] - 1 + 127, 0) - down, 1)
    scale = np.exp2(byte - 127.0)
    codes = (blocks / scale).astype(np.float32).astype(dtype).astype(np.float64)
    return np.moveaxis((codes * scale).reshape(v.shape), -1, axis)


WIDE = False


def mx_kscale(k):
    if not WIDE:
        return np.ones(k)
    levels = np.array([10, -10, 5, -5, 0])
    if k % 512:
        return np.exp2(np.random.permutation(np.resize(levels, k // 32))).repeat(32)
    a = np.empty((k // 512, 16))
    for p in range(k // 512):
        a[p, :8] = np.random.permutation(np.resize(levels, 8))
        for g in range(8):
            far = levels[np.abs(levels - a[p, g]) >= 10]
            a[p, g + 8] = far[np.random.randint(len(far))]
    return np.exp2(a.ravel()).repeat(32)


BF16 = ml_dtypes.bfloat16


def bf(x):
    return np.asarray(x, np.float32).astype(BF16)


def f64(x):
    return np.asarray(x).astype(np.float64)


B, N, E, F, H, K, C, G, DEG = 8, 512, 4096, 32, 64, 8, 16, 64, 8


def incidence(rows, cols):
    return (np.random.uniform(size=(rows, cols)) < DEG / N) * np.random.uniform(0.5, 1.5, (rows, cols))


def setup_inputs():
    s, t = mx_kscale(N), mx_kscale(E)
    return {"x": bf(np.random.standard_normal((B, N, C)) / s[None, :, None]),
            "rinc": bf(incidence(E, N) * s[None, :]),
            "linc": bf(incidence(N, E) * t[None, :]),
            "edge_w": bf(np.random.standard_normal((E, K)) * 0.25 / t[:, None])}


def reference(x, rinc, linc, edge_w):
    z = mxq(f64(rinc), 1, "e4m3") @ mxq(f64(x), 1, "e4m3")
    m = (z[:, :, :, None] * f64(edge_w)[None, :, None, :]).reshape(B, E, C * K)
    return mxq(f64(linc), 1, "e4m3") @ mxq(m, 1, "e4m3")

@@ -1,0 +1,213 @@
+from contextlib import ExitStack
+
+import concourse.mybir as mybir
+from concourse.masks import make_identity
+
+F32 = mybir.dt.float32
+BF16 = mybir.dt.bfloat16
+U32 = mybir.dt.uint32
+U8 = mybir.dt.uint8
+FP8X4 = mybir.dt.float8_e4m3fn_x4
+
+P = 128
+PACK = 4
+K_PASS = P * PACK
+
+SIGNALS, NODES, EDGES, CHANNELS, KERNELS = 8, 512, 4096, 16, 8
+PASSES = EDGES // K_PASS
+NODE_TILES = NODES // P
+ROUNDS = 2
+UNITS = ROUNDS * PASSES
+Z_COLS = SIGNALS * CHANNELS // ROUNDS
+M_COLS = Z_COLS * KERNELS
+WORDS = P
+SCALAR_KERNELS_FIRST_ROUND = 1
+SCALAR_KERNELS_LATER = 2
+RINC_LEAD = 2
+
+FLOPS = 2 * SIGNALS * EDGES * NODES * CHANNELS + 2 * SIGNALS * NODES * EDGES * CHANNELS * KERNELS
+
+
+def due(index, count):
+    return 0 <= index < count
+
+
+def tile_sgcn_pa_kernel(tc, x, rinc, linc, edge_w, out):
+    nc = tc.nc
+    with ExitStack() as stack:
+        keep = stack.enter_context(tc.tile_pool(name="keep", bufs=1))
+        stage = stack.enter_context(tc.tile_pool(name="stage", bufs=3))
+        results = stack.enter_context(tc.tile_pool(name="results", bufs=NODE_TILES))
+        work_banks = stack.enter_context(tc.psum_pool(name="work_banks", bufs=4))
+        y_banks = stack.enter_context(tc.psum_pool(name="y_banks", bufs=1))
+        stack.enter_context(tc.manual_schedule())
+
+        x_raw = keep.tile([P, SIGNALS, PACK, CHANNELS], BF16)
+        nc.scalar.dma_start(
+            out=x_raw[:].rearrange("q b s c -> q b (s c)"),
+            in_=x.rearrange("b (q s) c -> q b (s c)", s=PACK),
+        )
+        w_raw = keep.tile([P, PASSES * PACK * KERNELS], BF16)
+        nc.scalar.dma_start(
+            out=w_raw[:].rearrange("p (g tk) -> p g tk", g=PASSES),
+            in_=edge_w.rearrange("(g p t) k -> p g (t k)", p=P, t=PACK),
+        )
+        rinc_raw = []
+        linc_raw = []
+        for step in range(PASSES + RINC_LEAD):
+            if step < PASSES:
+                rows = keep.tile([P, PACK * NODES], BF16, name="rinc_raw%d" % step)
+                nc.sync.dma_start(
+                    out=rows[:],
+                    in_=rinc[K_PASS * step : K_PASS * (step + 1), :].rearrange("(p t) n -> p (t n)", t=PACK),
+                )
+                rinc_raw.append(rows)
+            if step >= RINC_LEAD:
+                g = step - RINC_LEAD
+                cols = keep.tile([P, NODE_TILES * K_PASS], BF16, name="linc_raw%d" % g)
+                nc.sync.dma_start(
+                    out=cols[:].rearrange("p (i e) -> p i e", i=NODE_TILES),
+                    in_=linc[:, K_PASS * g : K_PASS * (g + 1)].rearrange("(i p) e -> p i e", p=P),
+                )
+                linc_raw.append(cols)
+
+        ident = keep.tile([P, P], F32)
+        make_identity(nc, ident[:])
+
+        w_grouped = keep.tile([P, PASSES, KERNELS, PACK], F32)
+        nc.gpsimd.tensor_copy(
+            out=w_grouped[:],
+            in_=w_raw[:].rearrange("p (g t k) -> p g k t", g=PASSES, k=KERNELS),
+        )
+
+        x_codes = keep.tile([P, SIGNALS * CHANNELS], U32, align_bytes=64)
+        x_scales = keep.tile([P, SIGNALS * CHANNELS], U8, align_bytes=64)
+        rinc_codes = keep.tile([P, PASSES, K_PASS], U32, align_bytes=64)
+        rinc_scales = keep.tile([P, PASSES, K_PASS], U8, align_bytes=64)
+        linc_codes = keep.tile([P, PASSES, NODES], U32, align_bytes=64)
+        linc_scales = keep.tile([P, PASSES, NODES], U8, align_bytes=64)
+
+        x_grouped = keep.tile([P, SIGNALS * CHANNELS * PACK], BF16, align_bytes=64)
+        nc.vector.tensor_copy(
+            out=x_grouped[:].rearrange("q (b c s) -> q b c s", b=SIGNALS, s=PACK),
+            in_=x_raw[:].rearrange("q b s c -> q b c s"),
+        )
+        nc.vector.quantize_mx(out=x_codes[:].bitcast(FP8X4), scales=x_scales[:], in_=x_grouped[:])
+
+        grouped = {}
+        z = {}
+        m_codes = {}
+        m_scales = {}
+        y_acc = {}
+
+        def turn(name, g, raw):
+            raw_words = raw[:].bitcast(F32).rearrange("p (a w) -> p a w", a=4)
+            tile = stage.tile([P, PACK * K_PASS], BF16, name=name, align_bytes=64)
+            tile_words = tile[:].bitcast(F32).rearrange("p (a r u) -> p a r u", a=4, u=2)
+            for pair in range(2):
+                bank = work_banks.tile([P, 2, 2, WORDS], F32, tag="work")
+                for a in range(2):
+                    for u in range(2):
+                        nc.tensor.transpose(bank[:, a, u, :], raw_words[:, 2 * pair + a, u : 2 * WORDS : 2], ident[:])
+                nc.scalar.copy(
+                    out=tile_words[:, 2 * pair : 2 * pair + 2],
+                    in_=bank[:].rearrange("p a u r -> p a r u"),
+                )
+            grouped[name, g] = tile
+
+        def quantise(name, g, codes, scales):
+            nc.vector.quantize_mx(out=codes.bitcast(FP8X4), scales=scales, in_=grouped[name, g][:])
+
+        def first_matmul(unit):
+            r, g = divmod(unit, PASSES)
+            cols = slice(Z_COLS * r, Z_COLS * (r + 1))
+            z[unit] = work_banks.tile([P, PACK, Z_COLS], F32, name="z", tag="work")
+            for t in range(PACK):
+                rows = slice(P * t, P * (t + 1))
+                nc.tensor.matmul_mx(
+                    out=z[unit][:, t, :],
+                    lhsT=rinc_codes[:, g, rows].bitcast(FP8X4),
+                    lhsT_scale=rinc_scales[:, g, rows],
+                    rhs=x_codes[:, cols].bitcast(FP8X4),
+                    rhs_scale=x_scales[:, cols],
+                    start=True,
+                    stop=True,
+                )
+
+        def messages(unit):
+            r, g = divmod(unit, PASSES)
+            vector_kernels = KERNELS - (SCALAR_KERNELS_FIRST_ROUND if r == 0 else SCALAR_KERNELS_LATER)
+            tile = stage.tile([P, M_COLS * PACK], BF16, name="m_grouped", align_bytes=64)
+            planes = tile[:].rearrange("p (k c t) -> p k c t", k=KERNELS, t=PACK)
+            shape = [P, vector_kernels, Z_COLS, PACK]
+            nc.vector.tensor_tensor(
+                out=planes[:, :vector_kernels],
+                in0=z[unit][:].rearrange("p t c -> p c t").unsqueeze(1).to_broadcast(shape),
+                in1=w_grouped[:, g, :vector_kernels, :].unsqueeze(2).to_broadcast(shape),
+                op=mybir.AluOpType.mult,
+            )
+            for k in range(vector_kernels, KERNELS):
+                for t in range(PACK):
+                    nc.scalar.activation(
+                        out=planes[:, k, :, t],
+                        in_=z[unit][:, t, :],
+                        func=mybir.ActivationFunctionType.Copy,
+                        scale=w_grouped[:, g, k, t : t + 1],
+                    )
+            grouped["m", unit] = tile
+
+        def second_matmul(unit, node_tiles):
+            g = unit % PASSES
+            for i in node_tiles:
+                if g == 0:
+                    y_acc[i] = y_banks.tile([P, M_COLS], F32, name="y_acc%d" % i)
+                nodes = slice(P * i, P * (i + 1))
+                nc.tensor.matmul_mx(
+                    out=y_acc[i][:],
+                    lhsT=linc_codes[:, g, nodes].bitcast(FP8X4),
+                    lhsT_scale=linc_scales[:, g, nodes],
+                    rhs=m_codes[unit][:].bitcast(FP8X4),
+                    rhs_scale=m_scales[unit][:],
+                    start=(g == 0),
+                    stop=(g == PASSES - 1),
+                )
+
+        def store_round(r):
+            per_round = SIGNALS // ROUNDS
+            for i in range(NODE_TILES):
+                y_sb = results.tile([P, M_COLS], F32)
+                copy = nc.scalar.copy if i % 2 == 0 else nc.vector.tensor_copy
+                copy(
+                    out=y_sb[:].rearrange("p (c k) -> p c k", k=KERNELS),
+                    in_=y_acc[i][:].rearrange("p (k c) -> p c k", k=KERNELS),
+                )
+                nc.sync.dma_start(
+                    out=out[per_round * r : per_round * (r + 1), P * i : P * (i + 1), :].rearrange("b p j -> p b j"),
+                    in_=y_sb[:].rearrange("p (b j) -> p b j", b=per_round),
+                )
+
+        first_tiles = range(NODE_TILES // 2)
+        last_tiles = range(NODE_TILES // 2, NODE_TILES)
+        for u in range(-3, UNITS + 2):
+            if due(u, UNITS):
+                messages(u)
+            if due(u + 1, UNITS):
+                first_matmul(u + 1)
+            if due(u - 2, UNITS):
+                second_matmul(u - 2, first_tiles)
+            if due(u + 3, PASSES):
+                turn("rinc", u + 3, rinc_raw[u + 3])
+            if due(u + 2, PASSES):
+                quantise("rinc", u + 2, rinc_codes[:, u + 2, :], rinc_scales[:, u + 2, :])
+            if due(u, PASSES):
+                quantise("linc", u, linc_codes[:, u, :], linc_scales[:, u, :])
+            if due(u - 2, UNITS):
+                second_matmul(u - 2, last_tiles)
+                if (u - 2) % PASSES == PASSES - 1:
+                    store_round((u - 2) // PASSES)
+            if due(u + 1, PASSES):
+                turn("linc", u + 1, linc_raw[u + 1])
+            if due(u - 1, UNITS):
+                m_codes[u - 1] = stage.tile([P, M_COLS], U32, name="m_codes", align_bytes=64)
+                m_scales[u - 1] = stage.tile([P, M_COLS], U8, name="m_scales", align_bytes=64)
+                quantise("m", u - 1, m_codes[u - 1][:], m_scales[u - 1][:])

@@ -16,16 +16,24 @@ K_PASS = P * PACK
 SIGNALS, NODES, EDGES, CHANNELS, KERNELS = 8, 512, 4096, 16, 8
 PASSES = EDGES // K_PASS
 NODE_TILES = NODES // P
-ROUNDS = 2
-UNITS = ROUNDS * PASSES
-Z_COLS = SIGNALS * CHANNELS // ROUNDS
+HALVES = 2
+Z_COLS = SIGNALS * CHANNELS // HALVES
 M_COLS = Z_COLS * KERNELS
 WORDS = P
-SCALAR_KERNELS_FIRST_ROUND = 1
-SCALAR_KERNELS_LATER = 2
+SCALAR_KERNELS = 2
+VECTOR_KERNELS = KERNELS - SCALAR_KERNELS
+GPSIMD_COLS = 16
+VECTOR_COLS = Z_COLS - GPSIMD_COLS
 RINC_LEAD = 2
 
 FLOPS = 2 * SIGNALS * EDGES * NODES * CHANNELS + 2 * SIGNALS * NODES * EDGES * CHANNELS * KERNELS
+
+SPLIT = 3
+PAIRED = PASSES - SPLIT
+ORDER = [(g, h) for g in range(PAIRED) for h in range(HALVES)] + [
+    (g, h) for h in range(HALVES) for g in range(PAIRED, PASSES)
+]
+STEPS = len(ORDER)
 
 
 def due(index, count):
@@ -37,8 +45,10 @@ def tile_sgcn_pa_kernel(tc, x, rinc, linc, edge_w, out):
     with ExitStack() as stack:
         keep = stack.enter_context(tc.tile_pool(name="keep", bufs=1))
         stage = stack.enter_context(tc.tile_pool(name="stage", bufs=3))
-        results = stack.enter_context(tc.tile_pool(name="results", bufs=NODE_TILES))
-        work_banks = stack.enter_context(tc.psum_pool(name="work_banks", bufs=4))
+        codes = stack.enter_context(tc.tile_pool(name="codes", bufs=1))
+        results = stack.enter_context(tc.tile_pool(name="results", bufs=2 * NODE_TILES))
+        work_banks = stack.enter_context(tc.psum_pool(name="work_banks", bufs=2))
+        z_banks = stack.enter_context(tc.psum_pool(name="z_banks", bufs=2))
         y_banks = stack.enter_context(tc.psum_pool(name="y_banks", bufs=1))
         stack.enter_context(tc.manual_schedule())
 
@@ -96,6 +106,9 @@ def tile_sgcn_pa_kernel(tc, x, rinc, linc, edge_w, out):
 
         grouped = {}
         z = {}
+        z_gpsimd = {}
+        products = {}
+        to_prepare = {}
         m_codes = {}
         m_scales = {}
         y_acc = {}
@@ -105,7 +118,7 @@ def tile_sgcn_pa_kernel(tc, x, rinc, linc, edge_w, out):
             tile = stage.tile([P, PACK * K_PASS], BF16, name=name, align_bytes=64)
             tile_words = tile[:].bitcast(F32).rearrange("p (a r u) -> p a r u", a=4, u=2)
             for pair in range(2):
-                bank = work_banks.tile([P, 2, 2, WORDS], F32, tag="work")
+                bank = work_banks.tile([P, 2, 2, WORDS], F32, name="turned", tag="work")
                 for a in range(2):
                     for u in range(2):
                         nc.tensor.transpose(bank[:, a, u, :], raw_words[:, 2 * pair + a, u : 2 * WORDS : 2], ident[:])
@@ -115,17 +128,16 @@ def tile_sgcn_pa_kernel(tc, x, rinc, linc, edge_w, out):
                 )
             grouped[name, g] = tile
 
-        def quantise(name, g, codes, scales):
-            nc.vector.quantize_mx(out=codes.bitcast(FP8X4), scales=scales, in_=grouped[name, g][:])
+        def quantise(tile, codes_ap, scales_ap):
+            nc.vector.quantize_mx(out=codes_ap.bitcast(FP8X4), scales=scales_ap, in_=tile[:])
 
-        def first_matmul(unit):
-            r, g = divmod(unit, PASSES)
-            cols = slice(Z_COLS * r, Z_COLS * (r + 1))
-            z[unit] = work_banks.tile([P, PACK, Z_COLS], F32, name="z", tag="work")
+        def first_matmul(g, halves):
+            cols = slice(Z_COLS * halves[0], Z_COLS * (halves[-1] + 1))
+            tile = z_banks.tile([P, PACK, Z_COLS * len(halves)], F32, name="z")
             for t in range(PACK):
                 rows = slice(P * t, P * (t + 1))
                 nc.tensor.matmul_mx(
-                    out=z[unit][:, t, :],
+                    out=tile[:, t, :],
                     lhsT=rinc_codes[:, g, rows].bitcast(FP8X4),
                     lhsT_scale=rinc_scales[:, g, rows],
                     rhs=x_codes[:, cols].bitcast(FP8X4),
@@ -133,81 +145,142 @@ def tile_sgcn_pa_kernel(tc, x, rinc, linc, edge_w, out):
                     start=True,
                     stop=True,
                 )
+            for place, h in enumerate(halves):
+                z[g, h] = tile[:, :, Z_COLS * place : Z_COLS * (place + 1)]
+            return tile
 
-        def messages(unit):
-            r, g = divmod(unit, PASSES)
-            vector_kernels = KERNELS - (SCALAR_KERNELS_FIRST_ROUND if r == 0 else SCALAR_KERNELS_LATER)
-            tile = stage.tile([P, M_COLS * PACK], BF16, name="m_grouped", align_bytes=64)
-            planes = tile[:].rearrange("p (k c t) -> p k c t", k=KERNELS, t=PACK)
-            shape = [P, vector_kernels, Z_COLS, PACK]
-            nc.vector.tensor_tensor(
-                out=planes[:, :vector_kernels],
-                in0=z[unit][:].rearrange("p t c -> p c t").unsqueeze(1).to_broadcast(shape),
-                in1=w_grouped[:, g, :vector_kernels, :].unsqueeze(2).to_broadcast(shape),
-                op=mybir.AluOpType.mult,
+        def prepare(tile, g, halves):
+            for_gpsimd = stage.tile([P, len(halves), GPSIMD_COLS, PACK], F32, name="z_gpsimd")
+            nc.scalar.copy(
+                out=for_gpsimd[:],
+                in_=tile[:].rearrange("p t (h c) -> p h c t", c=Z_COLS)[:, :, VECTOR_COLS:, :],
             )
-            for k in range(vector_kernels, KERNELS):
+            runs = stage.tile([P, SCALAR_KERNELS, PACK, len(halves) * Z_COLS], BF16, name="products")
+            for k in range(SCALAR_KERNELS):
                 for t in range(PACK):
                     nc.scalar.activation(
-                        out=planes[:, k, :, t],
-                        in_=z[unit][:, t, :],
+                        out=runs[:, k, t, :],
+                        in_=tile[:, t, :],
                         func=mybir.ActivationFunctionType.Copy,
-                        scale=w_grouped[:, g, k, t : t + 1],
+                        scale=w_grouped[:, g, VECTOR_KERNELS + k, t : t + 1],
                     )
-            grouped["m", unit] = tile
+            for place, h in enumerate(halves):
+                z_gpsimd[g, h] = for_gpsimd[:, place]
+                products[g, h] = runs[:, :, :, Z_COLS * place : Z_COLS * (place + 1)]
 
-        def second_matmul(unit, node_tiles):
-            g = unit % PASSES
+        def messages(g, h):
+            tile = stage.tile([P, M_COLS * PACK], BF16, name="m_grouped", align_bytes=64)
+            planes = tile[:].rearrange("p (k c t) -> p k c t", k=KERNELS, t=PACK)
+            weights = w_grouped[:, g, :VECTOR_KERNELS, :].unsqueeze(2)
+            shape = [P, VECTOR_KERNELS, VECTOR_COLS, PACK]
+            nc.vector.tensor_tensor(
+                out=planes[:, :VECTOR_KERNELS, :VECTOR_COLS, :],
+                in0=z[g, h][:, :, :VECTOR_COLS].rearrange("p t c -> p c t").unsqueeze(1).to_broadcast(shape),
+                in1=weights.to_broadcast(shape),
+                op=mybir.AluOpType.mult,
+            )
+            shape = [P, VECTOR_KERNELS, GPSIMD_COLS, PACK]
+            nc.gpsimd.tensor_tensor(
+                out=planes[:, :VECTOR_KERNELS, VECTOR_COLS:, :],
+                in0=z_gpsimd[g, h].unsqueeze(1).to_broadcast(shape),
+                in1=weights.to_broadcast(shape),
+                op=mybir.AluOpType.mult,
+            )
+            nc.scalar.copy(
+                out=planes[:, VECTOR_KERNELS:, :, :],
+                in_=products[g, h].rearrange("p k t c -> p k c t"),
+            )
+            grouped["m", g, h] = tile
+
+        def quantise_messages(g, h):
+            m_codes[g, h] = codes.tile([P, M_COLS], U32, name="m_codes%d_%d" % (g, h), align_bytes=64)
+            m_scales[g, h] = codes.tile([P, M_COLS], U8, name="m_scales%d_%d" % (g, h), align_bytes=64)
+            quantise(grouped["m", g, h], m_codes[g, h][:], m_scales[g, h][:])
+
+        def second_matmul(g, h, node_tiles):
             for i in node_tiles:
                 if g == 0:
-                    y_acc[i] = y_banks.tile([P, M_COLS], F32, name="y_acc%d" % i)
+                    if h == 1 and i < 2:
+                        y_acc[h, i] = work_banks.tile([P, M_COLS], F32, name="y_late%d" % i, tag="work")
+                    else:
+                        place = i if h == 0 else i - 2
+                        y_acc[h, i] = y_banks.tile([P, M_COLS], F32, name="y%d_%d" % (h, i), tag="y%d" % place)
                 nodes = slice(P * i, P * (i + 1))
                 nc.tensor.matmul_mx(
-                    out=y_acc[i][:],
+                    out=y_acc[h, i][:],
                     lhsT=linc_codes[:, g, nodes].bitcast(FP8X4),
                     lhsT_scale=linc_scales[:, g, nodes],
-                    rhs=m_codes[unit][:].bitcast(FP8X4),
-                    rhs_scale=m_scales[unit][:],
+                    rhs=m_codes[g, h][:].bitcast(FP8X4),
+                    rhs_scale=m_scales[g, h][:],
                     start=(g == 0),
                     stop=(g == PASSES - 1),
                 )
 
-        def store_round(r):
-            per_round = SIGNALS // ROUNDS
-            for i in range(NODE_TILES):
+        def store_half(h, node_tiles):
+            signals = SIGNALS // HALVES
+            for i in node_tiles:
                 y_sb = results.tile([P, M_COLS], F32)
                 copy = nc.scalar.copy if i % 2 == 0 else nc.vector.tensor_copy
                 copy(
                     out=y_sb[:].rearrange("p (c k) -> p c k", k=KERNELS),
-                    in_=y_acc[i][:].rearrange("p (k c) -> p c k", k=KERNELS),
+                    in_=y_acc[h, i][:].rearrange("p (k c) -> p c k", k=KERNELS),
                 )
                 nc.sync.dma_start(
-                    out=out[per_round * r : per_round * (r + 1), P * i : P * (i + 1), :].rearrange("b p j -> p b j"),
-                    in_=y_sb[:].rearrange("p (b j) -> p b j", b=per_round),
+                    out=out[signals * h : signals * (h + 1), P * i : P * (i + 1), :].rearrange("b p j -> p b j"),
+                    in_=y_sb[:].rearrange("p (b j) -> p b j", b=signals),
                 )
 
-        first_tiles = range(NODE_TILES // 2)
-        last_tiles = range(NODE_TILES // 2, NODE_TILES)
-        for u in range(-3, UNITS + 2):
-            if due(u, UNITS):
-                messages(u)
-            if due(u + 1, UNITS):
-                first_matmul(u + 1)
-            if due(u - 2, UNITS):
-                second_matmul(u - 2, first_tiles)
-            if due(u + 3, PASSES):
-                turn("rinc", u + 3, rinc_raw[u + 3])
-            if due(u + 2, PASSES):
-                quantise("rinc", u + 2, rinc_codes[:, u + 2, :], rinc_scales[:, u + 2, :])
-            if due(u, PASSES):
-                quantise("linc", u, linc_codes[:, u, :], linc_scales[:, u, :])
-            if due(u - 2, UNITS):
-                second_matmul(u - 2, last_tiles)
-                if (u - 2) % PASSES == PASSES - 1:
-                    store_round((u - 2) // PASSES)
-            if due(u + 1, PASSES):
-                turn("linc", u + 1, linc_raw[u + 1])
-            if due(u - 1, UNITS):
-                m_codes[u - 1] = stage.tile([P, M_COLS], U32, name="m_codes", align_bytes=64)
-                m_scales[u - 1] = stage.tile([P, M_COLS], U8, name="m_scales", align_bytes=64)
-                quantise("m", u - 1, m_codes[u - 1][:], m_scales[u - 1][:])
+        all_tiles = range(NODE_TILES)
+        early_tiles = range(2)
+        late_tiles = range(2, NODE_TILES)
+
+        turn_rinc = {2 * (g - RINC_LEAD - 1): g for g in range(PASSES)}
+        quantise_rinc = {2 * (g - RINC_LEAD): g for g in range(PASSES)}
+        turn_linc = {min(2 * g - 1, g + PAIRED): g for g in range(PASSES)}
+        quantise_linc = {min(2 * g + 1, g + PAIRED + 1): g for g in range(PASSES)}
+        z_paired = {2 * (g - 1): g for g in range(PAIRED)}
+        z_single = {v - 2: ORDER[v] for v in range(2 * PAIRED, STEPS)}
+
+        for v in range(-2 * (RINC_LEAD + 1), STEPS):
+            if v in z_paired:
+                to_prepare[v + 1] = (first_matmul(z_paired[v], (0, 1)), z_paired[v], (0, 1))
+            if due(v, STEPS):
+                messages(*ORDER[v])
+            if v in to_prepare:
+                prepare(*to_prepare[v])
+            if v in turn_rinc:
+                g = turn_rinc[v]
+                turn("rinc", g, rinc_raw[g])
+            if v in quantise_rinc:
+                g = quantise_rinc[v]
+                quantise(grouped["rinc", g], rinc_codes[:, g, :], rinc_scales[:, g, :])
+            if v in quantise_linc:
+                g = quantise_linc[v]
+                quantise(grouped["linc", g], linc_codes[:, g, :], linc_scales[:, g, :])
+            if v in turn_linc:
+                g = turn_linc[v]
+                turn("linc", g, linc_raw[g])
+            if due(v - 1, STEPS):
+                quantise_messages(*ORDER[v - 1])
+            if due(v - 2, STEPS):
+                g, h = ORDER[v - 2]
+                if h == 0:
+                    second_matmul(g, 0, all_tiles)
+            if v == STEPS - 3:
+                for g in range(3):
+                    second_matmul(g, 1, early_tiles)
+            if v == STEPS - 2:
+                store_half(0, all_tiles)
+                for g in range(3, PAIRED):
+                    second_matmul(g, 1, early_tiles)
+            if v == STEPS - 1:
+                for g in range(PAIRED):
+                    second_matmul(g, 1, late_tiles)
+                second_matmul(PAIRED, 1, all_tiles)
+            if v in z_single:
+                g, h = z_single[v]
+                to_prepare[v + 1] = (first_matmul(g, (h,)), g, (h,))
+        quantise_messages(*ORDER[STEPS - 1])
+        for g in range(PAIRED + 1, PASSES):
+            second_matmul(g, 1, all_tiles)
+        store_half(1, all_tiles)

@@ -20,15 +20,15 @@ HALVES = 2
 Z_COLS = SIGNALS * CHANNELS // HALVES
 M_COLS = Z_COLS * KERNELS
 WORDS = P
+SCALAR_FROM = 2
 SCALAR_KERNELS = 2
-VECTOR_KERNELS = KERNELS - SCALAR_KERNELS
 GPSIMD_COLS = 16
 VECTOR_COLS = Z_COLS - GPSIMD_COLS
-RINC_LEAD = 2
+BANKS = 6
 
 FLOPS = 2 * SIGNALS * EDGES * NODES * CHANNELS + 2 * SIGNALS * NODES * EDGES * CHANNELS * KERNELS
 
-SPLIT = 3
+SPLIT = 5
 PAIRED = PASSES - SPLIT
 ORDER = [(g, h) for g in range(PAIRED) for h in range(HALVES)] + [
     (g, h) for h in range(HALVES) for g in range(PAIRED, PASSES)
@@ -36,8 +36,8 @@ ORDER = [(g, h) for g in range(PAIRED) for h in range(HALVES)] + [
 STEPS = len(ORDER)
 
 
-def due(index, count):
-    return 0 <= index < count
+def scalar_kernels(g):
+    return SCALAR_KERNELS if g >= SCALAR_FROM else 0
 
 
 def tile_sgcn_pa_kernel(tc, x, rinc, linc, edge_w, out):
@@ -47,9 +47,8 @@ def tile_sgcn_pa_kernel(tc, x, rinc, linc, edge_w, out):
         stage = stack.enter_context(tc.tile_pool(name="stage", bufs=3))
         codes = stack.enter_context(tc.tile_pool(name="codes", bufs=1))
         results = stack.enter_context(tc.tile_pool(name="results", bufs=2 * NODE_TILES))
-        work_banks = stack.enter_context(tc.psum_pool(name="work_banks", bufs=2))
+        banks = stack.enter_context(tc.psum_pool(name="banks", bufs=1))
         z_banks = stack.enter_context(tc.psum_pool(name="z_banks", bufs=2))
-        y_banks = stack.enter_context(tc.psum_pool(name="y_banks", bufs=1))
         stack.enter_context(tc.manual_schedule())
 
         x_raw = keep.tile([P, SIGNALS, PACK, CHANNELS], BF16)
@@ -63,23 +62,22 @@ def tile_sgcn_pa_kernel(tc, x, rinc, linc, edge_w, out):
             in_=edge_w.rearrange("(g p t) k -> p g (t k)", p=P, t=PACK),
         )
         rinc_raw = []
+        for g in range(PASSES):
+            rows = keep.tile([P, PACK, NODES], BF16, name="rinc_raw%d" % g)
+            source = rinc[K_PASS * g : K_PASS * (g + 1), :].rearrange("(p t) n -> p t n", t=PACK)
+            pieces = 2 if g == 0 else 1
+            for piece in range(pieces):
+                part = slice(PACK // pieces * piece, PACK // pieces * (piece + 1))
+                nc.sync.dma_start(out=rows[:, part, :], in_=source[:, part, :])
+            rinc_raw.append(rows[:].rearrange("p t n -> p (t n)"))
         linc_raw = []
-        for step in range(PASSES + RINC_LEAD):
-            if step < PASSES:
-                rows = keep.tile([P, PACK * NODES], BF16, name="rinc_raw%d" % step)
-                nc.sync.dma_start(
-                    out=rows[:],
-                    in_=rinc[K_PASS * step : K_PASS * (step + 1), :].rearrange("(p t) n -> p (t n)", t=PACK),
-                )
-                rinc_raw.append(rows)
-            if step >= RINC_LEAD:
-                g = step - RINC_LEAD
-                cols = keep.tile([P, NODE_TILES * K_PASS], BF16, name="linc_raw%d" % g)
-                nc.sync.dma_start(
-                    out=cols[:].rearrange("p (i e) -> p i e", i=NODE_TILES),
-                    in_=linc[:, K_PASS * g : K_PASS * (g + 1)].rearrange("(i p) e -> p i e", p=P),
-                )
-                linc_raw.append(cols)
+        for g in range(PASSES):
+            cols = keep.tile([P, NODE_TILES * K_PASS], BF16, name="linc_raw%d" % g)
+            nc.sync.dma_start(
+                out=cols[:].rearrange("p (i e) -> p i e", i=NODE_TILES),
+                in_=linc[:, K_PASS * g : K_PASS * (g + 1)].rearrange("(i p) e -> p i e", p=P),
+            )
+            linc_raw.append(cols[:])
 
         ident = keep.tile([P, P], F32)
         make_identity(nc, ident[:])
@@ -113,12 +111,20 @@ def tile_sgcn_pa_kernel(tc, x, rinc, linc, edge_w, out):
         m_scales = {}
         y_acc = {}
 
+        banks_used = []
+
+        def next_bank(shape):
+            place = len(banks_used) % BANKS
+            bank = banks.tile(shape, F32, name="bank%d" % place)
+            banks_used.append(place)
+            return bank
+
         def turn(name, g, raw):
-            raw_words = raw[:].bitcast(F32).rearrange("p (a w) -> p a w", a=4)
-            tile = stage.tile([P, PACK * K_PASS], BF16, name=name, align_bytes=64)
+            raw_words = raw.bitcast(F32).rearrange("p (a w) -> p a w", a=4)
+            tile = stage.tile([P, PACK * K_PASS], BF16, name="turned", bufs=5, align_bytes=64)
             tile_words = tile[:].bitcast(F32).rearrange("p (a r u) -> p a r u", a=4, u=2)
             for pair in range(2):
-                bank = work_banks.tile([P, 2, 2, WORDS], F32, name="turned", tag="work")
+                bank = next_bank([P, 2, 2, WORDS])
                 for a in range(2):
                     for u in range(2):
                         nc.tensor.transpose(bank[:, a, u, :], raw_words[:, 2 * pair + a, u : 2 * WORDS : 2], ident[:])
@@ -155,41 +161,48 @@ def tile_sgcn_pa_kernel(tc, x, rinc, linc, edge_w, out):
                 out=for_gpsimd[:],
                 in_=tile[:].rearrange("p t (h c) -> p h c t", c=Z_COLS)[:, :, VECTOR_COLS:, :],
             )
-            runs = stage.tile([P, SCALAR_KERNELS, PACK, len(halves) * Z_COLS], BF16, name="products")
-            for k in range(SCALAR_KERNELS):
+            for place, h in enumerate(halves):
+                z_gpsimd[g, h] = for_gpsimd[:, place]
+            mine = scalar_kernels(g)
+            if mine == 0:
+                return
+            runs = stage.tile([P, mine, PACK, len(halves) * Z_COLS], BF16, name="products")
+            for k in range(mine):
                 for t in range(PACK):
+                    k_all = KERNELS - mine + k
                     nc.scalar.activation(
                         out=runs[:, k, t, :],
                         in_=tile[:, t, :],
                         func=mybir.ActivationFunctionType.Copy,
-                        scale=w_grouped[:, g, VECTOR_KERNELS + k, t : t + 1],
+                        scale=w_grouped[:, g, k_all, t : t + 1],
                     )
             for place, h in enumerate(halves):
-                z_gpsimd[g, h] = for_gpsimd[:, place]
                 products[g, h] = runs[:, :, :, Z_COLS * place : Z_COLS * (place + 1)]
 
         def messages(g, h):
             tile = stage.tile([P, M_COLS * PACK], BF16, name="m_grouped", align_bytes=64)
             planes = tile[:].rearrange("p (k c t) -> p k c t", k=KERNELS, t=PACK)
-            weights = w_grouped[:, g, :VECTOR_KERNELS, :].unsqueeze(2)
-            shape = [P, VECTOR_KERNELS, VECTOR_COLS, PACK]
+            others = KERNELS - scalar_kernels(g)
+            weights = w_grouped[:, g, :others, :].unsqueeze(2)
+            shape = [P, others, VECTOR_COLS, PACK]
             nc.vector.tensor_tensor(
-                out=planes[:, :VECTOR_KERNELS, :VECTOR_COLS, :],
+                out=planes[:, :others, :VECTOR_COLS, :],
                 in0=z[g, h][:, :, :VECTOR_COLS].rearrange("p t c -> p c t").unsqueeze(1).to_broadcast(shape),
                 in1=weights.to_broadcast(shape),
                 op=mybir.AluOpType.mult,
             )
-            shape = [P, VECTOR_KERNELS, GPSIMD_COLS, PACK]
+            shape = [P, others, GPSIMD_COLS, PACK]
             nc.gpsimd.tensor_tensor(
-                out=planes[:, :VECTOR_KERNELS, VECTOR_COLS:, :],
+                out=planes[:, :others, VECTOR_COLS:, :],
                 in0=z_gpsimd[g, h].unsqueeze(1).to_broadcast(shape),
                 in1=weights.to_broadcast(shape),
                 op=mybir.AluOpType.mult,
             )
-            nc.scalar.copy(
-                out=planes[:, VECTOR_KERNELS:, :, :],
-                in_=products[g, h].rearrange("p k t c -> p k c t"),
-            )
+            if others < KERNELS:
+                nc.scalar.copy(
+                    out=planes[:, others:, :, :],
+                    in_=products[g, h].rearrange("p k t c -> p k c t"),
+                )
             grouped["m", g, h] = tile
 
         def quantise_messages(g, h):
@@ -200,11 +213,7 @@ def tile_sgcn_pa_kernel(tc, x, rinc, linc, edge_w, out):
         def second_matmul(g, h, node_tiles):
             for i in node_tiles:
                 if g == 0:
-                    if h == 1 and i < 2:
-                        y_acc[h, i] = work_banks.tile([P, M_COLS], F32, name="y_late%d" % i, tag="work")
-                    else:
-                        place = i if h == 0 else i - 2
-                        y_acc[h, i] = y_banks.tile([P, M_COLS], F32, name="y%d_%d" % (h, i), tag="y%d" % place)
+                    y_acc[h, i] = next_bank([P, M_COLS])
                 nodes = slice(P * i, P * (i + 1))
                 nc.tensor.matmul_mx(
                     out=y_acc[h, i][:],
@@ -231,56 +240,57 @@ def tile_sgcn_pa_kernel(tc, x, rinc, linc, edge_w, out):
                 )
 
         all_tiles = range(NODE_TILES)
-        early_tiles = range(2)
-        late_tiles = range(2, NODE_TILES)
+        early_tiles = range(BANKS - NODE_TILES)
+        late_tiles = range(BANKS - NODE_TILES, NODE_TILES)
+        to_turn = [("rinc", g, rinc_raw, rinc_codes, rinc_scales) for g in range(PASSES)] + [
+            ("linc", g, linc_raw, linc_codes, linc_scales) for g in range(PASSES)
+        ]
+        turns = {}
+        quantises = {}
+        for n, what in enumerate(to_turn):
+            turns.setdefault((n - 3) // 4, []).append(what)
+            quantises.setdefault((n - 2) // 4, []).append(what)
+        y_from = 4
+        z_paired = {2 * g - 1: g for g in range(PAIRED)}
+        z_single = {w - 2: ORDER[w] for w in range(2 * PAIRED, STEPS)}
+        to_prepare = {}
+        last_early = ORDER.index((PASSES - 1, 0)) + 2
 
-        turn_rinc = {2 * (g - RINC_LEAD - 1): g for g in range(PASSES)}
-        quantise_rinc = {2 * (g - RINC_LEAD): g for g in range(PASSES)}
-        turn_linc = {min(2 * g - 1, g + PAIRED): g for g in range(PASSES)}
-        quantise_linc = {min(2 * g + 1, g + PAIRED + 1): g for g in range(PASSES)}
-        z_paired = {2 * (g - 1): g for g in range(PAIRED)}
-        z_single = {v - 2: ORDER[v] for v in range(2 * PAIRED, STEPS)}
+        def sums(w):
+            g, h = ORDER[w]
+            second_matmul(g, h, all_tiles if h == 0 or w + 2 > last_early + 1 else early_tiles)
 
-        for v in range(-2 * (RINC_LEAD + 1), STEPS):
-            if v in z_paired:
-                to_prepare[v + 1] = (first_matmul(z_paired[v], (0, 1)), z_paired[v], (0, 1))
-            if due(v, STEPS):
-                messages(*ORDER[v])
+        for v in range(-1, STEPS):
+            if v >= 0 and v in z_paired:
+                prepare(first_matmul(z_paired[v], (0, 1)), z_paired[v], (0, 1))
             if v in to_prepare:
                 prepare(*to_prepare[v])
-            if v in turn_rinc:
-                g = turn_rinc[v]
-                turn("rinc", g, rinc_raw[g])
-            if v in quantise_rinc:
-                g = quantise_rinc[v]
-                quantise(grouped["rinc", g], rinc_codes[:, g, :], rinc_scales[:, g, :])
-            if v in quantise_linc:
-                g = quantise_linc[v]
-                quantise(grouped["linc", g], linc_codes[:, g, :], linc_scales[:, g, :])
-            if v in turn_linc:
-                g = turn_linc[v]
-                turn("linc", g, linc_raw[g])
-            if due(v - 1, STEPS):
+            for name, g, raw, codes_all, scales_all in turns.get(v, ()):
+                turn(name, g, raw[g])
+            if v >= 0:
+                messages(*ORDER[v])
+            for name, g, raw, codes_all, scales_all in quantises.get(v, ()):
+                quantise(grouped[name, g], codes_all[:, g, :], scales_all[:, g, :])
+            if v >= 1:
                 quantise_messages(*ORDER[v - 1])
-            if due(v - 2, STEPS):
-                g, h = ORDER[v - 2]
-                if h == 0:
-                    second_matmul(g, 0, all_tiles)
-            if v == STEPS - 3:
-                for g in range(3):
-                    second_matmul(g, 1, early_tiles)
-            if v == STEPS - 2:
+            if v == y_from:
+                for w in range(v - 2):
+                    sums(w)
+            if v >= y_from:
+                sums(v - 2)
+            if v == last_early:
                 store_half(0, all_tiles)
-                for g in range(3, PAIRED):
-                    second_matmul(g, 1, early_tiles)
-            if v == STEPS - 1:
-                for g in range(PAIRED):
-                    second_matmul(g, 1, late_tiles)
-                second_matmul(PAIRED, 1, all_tiles)
+            if v == last_early + 1:
+                for w in range(v - 1):
+                    g, h = ORDER[w]
+                    if h == 1:
+                        second_matmul(g, h, late_tiles)
+            if v == -1:
+                prepare(first_matmul(0, (0, 1)), 0, (0, 1))
             if v in z_single:
                 g, h = z_single[v]
                 to_prepare[v + 1] = (first_matmul(g, (h,)), g, (h,))
         quantise_messages(*ORDER[STEPS - 1])
-        for g in range(PAIRED + 1, PASSES):
-            second_matmul(g, 1, all_tiles)
+        for w in range(STEPS - 2, STEPS):
+            sums(w)
         store_half(1, all_tiles)

@@ -21,9 +21,10 @@ Z_COLS = SIGNALS * CHANNELS // HALVES
 M_COLS = Z_COLS * KERNELS
 WORDS = P
 SCALAR_FROM = 2
-SCALAR_KERNELS = 2
+SCALAR_KERNELS = (3, 2)
 GPSIMD_COLS = 16
 VECTOR_COLS = Z_COLS - GPSIMD_COLS
+RUN = 4
 BANKS = 6
 
 FLOPS = 2 * SIGNALS * EDGES * NODES * CHANNELS + 2 * SIGNALS * NODES * EDGES * CHANNELS * KERNELS
@@ -36,8 +37,8 @@ ORDER = [(g, h) for g in range(PAIRED) for h in range(HALVES)] + [
 STEPS = len(ORDER)
 
 
-def scalar_kernels(g):
-    return SCALAR_KERNELS if g >= SCALAR_FROM else 0
+def scalar_kernels(g, h):
+    return SCALAR_KERNELS[h] if g >= SCALAR_FROM else 0
 
 
 def tile_sgcn_pa_kernel(tc, x, rinc, linc, edge_w, out):
@@ -51,16 +52,6 @@ def tile_sgcn_pa_kernel(tc, x, rinc, linc, edge_w, out):
         z_banks = stack.enter_context(tc.psum_pool(name="z_banks", bufs=2))
         stack.enter_context(tc.manual_schedule())
 
-        x_raw = keep.tile([P, SIGNALS, PACK, CHANNELS], BF16)
-        nc.scalar.dma_start(
-            out=x_raw[:].rearrange("q b s c -> q b (s c)"),
-            in_=x.rearrange("b (q s) c -> q b (s c)", s=PACK),
-        )
-        w_raw = keep.tile([P, PASSES * PACK * KERNELS], BF16)
-        nc.scalar.dma_start(
-            out=w_raw[:].rearrange("p (g tk) -> p g tk", g=PASSES),
-            in_=edge_w.rearrange("(g p t) k -> p g (t k)", p=P, t=PACK),
-        )
         rinc_raw = []
         for g in range(PASSES):
             rows = keep.tile([P, PACK, NODES], BF16, name="rinc_raw%d" % g)
@@ -70,6 +61,17 @@ def tile_sgcn_pa_kernel(tc, x, rinc, linc, edge_w, out):
                 part = slice(PACK // pieces * piece, PACK // pieces * (piece + 1))
                 nc.sync.dma_start(out=rows[:, part, :], in_=source[:, part, :])
             rinc_raw.append(rows[:].rearrange("p t n -> p (t n)"))
+            if g == 0:
+                x_raw = keep.tile([P, SIGNALS, PACK, CHANNELS], BF16)
+                nc.sync.dma_start(
+                    out=x_raw[:].rearrange("q b s c -> q b (s c)"),
+                    in_=x.rearrange("b (q s) c -> q b (s c)", s=PACK),
+                )
+                w_raw = keep.tile([P, PASSES * PACK * KERNELS], BF16)
+                nc.sync.dma_start(
+                    out=w_raw[:].rearrange("p (g tk) -> p g tk", g=PASSES),
+                    in_=edge_w.rearrange("(g p t) k -> p g (t k)", p=P, t=PACK),
+                )
         linc_raw = []
         for g in range(PASSES):
             cols = keep.tile([P, NODE_TILES * K_PASS], BF16, name="linc_raw%d" % g)
@@ -163,26 +165,27 @@ def tile_sgcn_pa_kernel(tc, x, rinc, linc, edge_w, out):
             )
             for place, h in enumerate(halves):
                 z_gpsimd[g, h] = for_gpsimd[:, place]
-            mine = scalar_kernels(g)
-            if mine == 0:
+            mine = [scalar_kernels(g, h) for h in halves]
+            if max(mine) == 0:
                 return
-            runs = stage.tile([P, mine, PACK, len(halves) * Z_COLS], BF16, name="products")
-            for k in range(mine):
+            most = max(mine)
+            runs = stage.tile([P, PACK, len(halves), most, Z_COLS], BF16, name="products")
+            for k in range(most):
+                count = len([1 for number in mine if k >= most - number])
                 for t in range(PACK):
-                    k_all = KERNELS - mine + k
                     nc.scalar.activation(
-                        out=runs[:, k, t, :],
-                        in_=tile[:, t, :],
+                        out=runs[:, t, :count, k, :],
+                        in_=tile[:, t, : count * Z_COLS].rearrange("p (h c) -> p h c", h=count),
                         func=mybir.ActivationFunctionType.Copy,
-                        scale=w_grouped[:, g, k_all, t : t + 1],
+                        scale=w_grouped[:, g, KERNELS - most + k, t : t + 1],
                     )
             for place, h in enumerate(halves):
-                products[g, h] = runs[:, :, :, Z_COLS * place : Z_COLS * (place + 1)]
+                products[g, h] = runs[:, :, place, most - mine[place] :, :]
 
         def messages(g, h):
             tile = stage.tile([P, M_COLS * PACK], BF16, name="m_grouped", align_bytes=64)
             planes = tile[:].rearrange("p (k c t) -> p k c t", k=KERNELS, t=PACK)
-            others = KERNELS - scalar_kernels(g)
+            others = KERNELS - scalar_kernels(g, h)
             weights = w_grouped[:, g, :others, :].unsqueeze(2)
             shape = [P, others, VECTOR_COLS, PACK]
             nc.vector.tensor_tensor(
@@ -200,8 +203,8 @@ def tile_sgcn_pa_kernel(tc, x, rinc, linc, edge_w, out):
             )
             if others < KERNELS:
                 nc.scalar.copy(
-                    out=planes[:, others:, :, :],
-                    in_=products[g, h].rearrange("p k t c -> p k c t"),
+                    out=tile[:, others * Z_COLS * PACK :].rearrange("p (b i t) -> p b t i", i=RUN, t=PACK),
+                    in_=products[g, h].rearrange("p t k c -> p t (k c)").rearrange("p t (b i) -> p b t i", i=RUN),
                 )
             grouped["m", g, h] = tile
 
@@ -248,8 +251,8 @@ def tile_sgcn_pa_kernel(tc, x, rinc, linc, edge_w, out):
         turns = {}
         quantises = {}
         for n, what in enumerate(to_turn):
-            turns.setdefault((n - 3) // 4, []).append(what)
-            quantises.setdefault((n - 2) // 4, []).append(what)
+            turns.setdefault((n - 2) // 4, []).append(what)
+            quantises.setdefault((n - 1) // 4, []).append(what)
         y_from = 4
         z_paired = {2 * g - 1: g for g in range(PAIRED)}
         z_single = {w - 2: ORDER[w] for w in range(2 * PAIRED, STEPS)}
@@ -267,29 +270,34 @@ def tile_sgcn_pa_kernel(tc, x, rinc, linc, edge_w, out):
                 prepare(*to_prepare[v])
             for name, g, raw, codes_all, scales_all in turns.get(v, ()):
                 turn(name, g, raw[g])
+            if v == STEPS - 1:
+                quantise_messages(*ORDER[v - 1])
             if v >= 0:
                 messages(*ORDER[v])
             for name, g, raw, codes_all, scales_all in quantises.get(v, ()):
                 quantise(grouped[name, g], codes_all[:, g, :], scales_all[:, g, :])
-            if v >= 1:
+            if 1 <= v < STEPS - 1:
                 quantise_messages(*ORDER[v - 1])
-            if v == y_from:
-                for w in range(v - 2):
-                    sums(w)
-            if v >= y_from:
-                sums(v - 2)
-            if v == last_early:
-                store_half(0, all_tiles)
-            if v == last_early + 1:
-                for w in range(v - 1):
-                    g, h = ORDER[w]
-                    if h == 1:
-                        second_matmul(g, h, late_tiles)
-            if v == -1:
-                prepare(first_matmul(0, (0, 1)), 0, (0, 1))
-            if v in z_single:
+            due = list(range(v - 1)) if v == y_from else [v - 2] if v > y_from else []
+            for w in due[:1]:
+                sums(w)
+            if v in z_single and v <= last_early:
                 g, h = z_single[v]
                 to_prepare[v + 1] = (first_matmul(g, (h,)), g, (h,))
+            for w in due[1:]:
+                sums(w)
+            if v == last_early:
+                store_half(0, all_tiles)
+            late = [ORDER[w] for w in range(v - 1) if ORDER[w][1] == 1] if v == last_early + 1 else []
+            for g, h in late[:2]:
+                second_matmul(g, h, late_tiles)
+            if v > last_early and v in z_single:
+                g, h = z_single[v]
+                to_prepare[v + 1] = (first_matmul(g, (h,)), g, (h,))
+            for g, h in late[2:]:
+                second_matmul(g, h, late_tiles)
+            if v == -1:
+                prepare(first_matmul(0, (0, 1)), 0, (0, 1))
         quantise_messages(*ORDER[STEPS - 1])
         for w in range(STEPS - 2, STEPS):
             sums(w)

@@ -29,7 +29,7 @@ BANKS = 6
 
 FLOPS = 2 * SIGNALS * EDGES * NODES * CHANNELS + 2 * SIGNALS * NODES * EDGES * CHANNELS * KERNELS
 
-SPLIT = 5
+SPLIT = 4
 PAIRED = PASSES - SPLIT
 ORDER = [(g, h) for g in range(PAIRED) for h in range(HALVES)] + [
     (g, h) for h in range(HALVES) for g in range(PAIRED, PASSES)
@@ -123,7 +123,7 @@ def tile_sgcn_pa_kernel(tc, x, rinc, linc, edge_w, out):
 
         def turn(name, g, raw):
             raw_words = raw.bitcast(F32).rearrange("p (a w) -> p a w", a=4)
-            tile = stage.tile([P, PACK * K_PASS], BF16, name="turned", bufs=5, align_bytes=64)
+            tile = stage.tile([P, PACK * K_PASS], BF16, name="turned", bufs=8, align_bytes=64)
             tile_words = tile[:].bitcast(F32).rearrange("p (a r u) -> p a r u", a=4, u=2)
             for pair in range(2):
                 bank = next_bank([P, 2, 2, WORDS])
@@ -234,8 +234,8 @@ def tile_sgcn_pa_kernel(tc, x, rinc, linc, edge_w, out):
                 y_sb = results.tile([P, M_COLS], F32)
                 copy = nc.scalar.copy if i % 2 == 0 else nc.vector.tensor_copy
                 copy(
-                    out=y_sb[:].rearrange("p (c k) -> p c k", k=KERNELS),
-                    in_=y_acc[h, i][:].rearrange("p (k c) -> p c k", k=KERNELS),
+                    out=y_sb[:].rearrange("p (c s k) -> p s c k", s=2, k=KERNELS // 2),
+                    in_=y_acc[h, i][:].rearrange("p (s k c) -> p s c k", s=2, k=KERNELS // 2),
                 )
                 nc.sync.dma_start(
                     out=out[signals * h : signals * (h + 1), P * i : P * (i + 1), :].rearrange("b p j -> p b j"),
@@ -252,7 +252,7 @@ def tile_sgcn_pa_kernel(tc, x, rinc, linc, edge_w, out):
         quantises = {}
         for n, what in enumerate(to_turn):
             turns.setdefault((n - 2) // 4, []).append(what)
-            quantises.setdefault((n - 1) // 4, []).append(what)
+            quantises.setdefault((n - 1) // 3, []).append(what)
         y_from = 4
         z_paired = {2 * g - 1: g for g in range(PAIRED)}
         z_single = {w - 2: ORDER[w] for w in range(2 * PAIRED, STEPS)}

@@ -26,6 +26,9 @@ GPSIMD_COLS = 16
 VECTOR_COLS = Z_COLS - GPSIMD_COLS
 RUN = 4
 BANKS = 6
+TURNED_A_STEP = 4
+QUANTISED_A_STEP = 3
+TURNED_BUFS = 8
 
 FLOPS = 2 * SIGNALS * EDGES * NODES * CHANNELS + 2 * SIGNALS * NODES * EDGES * CHANNELS * KERNELS
 
@@ -52,6 +55,8 @@ def tile_sgcn_pa_kernel(tc, x, rinc, linc, edge_w, out):
         z_banks = stack.enter_context(tc.psum_pool(name="z_banks", bufs=2))
         stack.enter_context(tc.manual_schedule())
 
+        x_raw = keep.tile([P, SIGNALS, PACK, CHANNELS], BF16)
+        w_raw = keep.tile([P, PASSES * PACK * KERNELS], BF16)
         rinc_raw = []
         for g in range(PASSES):
             rows = keep.tile([P, PACK, NODES], BF16, name="rinc_raw%d" % g)
@@ -61,13 +66,12 @@ def tile_sgcn_pa_kernel(tc, x, rinc, linc, edge_w, out):
                 part = slice(PACK // pieces * piece, PACK // pieces * (piece + 1))
                 nc.sync.dma_start(out=rows[:, part, :], in_=source[:, part, :])
             rinc_raw.append(rows[:].rearrange("p t n -> p (t n)"))
-            if g == 0:
-                x_raw = keep.tile([P, SIGNALS, PACK, CHANNELS], BF16)
+            if g == 1:
                 nc.sync.dma_start(
                     out=x_raw[:].rearrange("q b s c -> q b (s c)"),
                     in_=x.rearrange("b (q s) c -> q b (s c)", s=PACK),
                 )
-                w_raw = keep.tile([P, PASSES * PACK * KERNELS], BF16)
+            if g == 2:
                 nc.sync.dma_start(
                     out=w_raw[:].rearrange("p (g tk) -> p g tk", g=PASSES),
                     in_=edge_w.rearrange("(g p t) k -> p g (t k)", p=P, t=PACK),
@@ -108,11 +112,9 @@ def tile_sgcn_pa_kernel(tc, x, rinc, linc, edge_w, out):
         z = {}
         z_gpsimd = {}
         products = {}
-        to_prepare = {}
         m_codes = {}
         m_scales = {}
         y_acc = {}
-
         banks_used = []
 
         def next_bank(shape):
@@ -123,7 +125,7 @@ def tile_sgcn_pa_kernel(tc, x, rinc, linc, edge_w, out):
 
         def turn(name, g, raw):
             raw_words = raw.bitcast(F32).rearrange("p (a w) -> p a w", a=4)
-            tile = stage.tile([P, PACK * K_PASS], BF16, name="turned", bufs=8, align_bytes=64)
+            tile = stage.tile([P, PACK * K_PASS], BF16, name="turned", bufs=TURNED_BUFS, align_bytes=64)
             tile_words = tile[:].bitcast(F32).rearrange("p (a r u) -> p a r u", a=4, u=2)
             for pair in range(2):
                 bank = next_bank([P, 2, 2, WORDS])
@@ -166,9 +168,9 @@ def tile_sgcn_pa_kernel(tc, x, rinc, linc, edge_w, out):
             for place, h in enumerate(halves):
                 z_gpsimd[g, h] = for_gpsimd[:, place]
             mine = [scalar_kernels(g, h) for h in halves]
-            if max(mine) == 0:
-                return
             most = max(mine)
+            if most == 0:
+                return
             runs = stage.tile([P, PACK, len(halves), most, Z_COLS], BF16, name="products")
             for k in range(most):
                 count = len([1 for number in mine if k >= most - number])
@@ -251,21 +253,21 @@ def tile_sgcn_pa_kernel(tc, x, rinc, linc, edge_w, out):
         turns = {}
         quantises = {}
         for n, what in enumerate(to_turn):
-            turns.setdefault((n - 2) // 4, []).append(what)
-            quantises.setdefault((n - 1) // 3, []).append(what)
-        y_from = 4
-        z_paired = {2 * g - 1: g for g in range(PAIRED)}
-        z_single = {w - 2: ORDER[w] for w in range(2 * PAIRED, STEPS)}
+            turns.setdefault((n - 2) // TURNED_A_STEP, []).append(what)
+            quantises.setdefault((n - 1) // QUANTISED_A_STEP, []).append(what)
+        sums_from = max(turns) + 1
+        first_half_done = ORDER.index((PASSES - 1, 0)) + 2
+        paired_z = {2 * g - 1: g for g in range(1, PAIRED)}
+        single_z = {made - 2: ORDER[made] for made in range(2 * PAIRED, STEPS)}
         to_prepare = {}
-        last_early = ORDER.index((PASSES - 1, 0)) + 2
 
-        def sums(w):
-            g, h = ORDER[w]
-            second_matmul(g, h, all_tiles if h == 0 or w + 2 > last_early + 1 else early_tiles)
+        def sums(made):
+            g, h = ORDER[made]
+            second_matmul(g, h, all_tiles if h == 0 or made >= first_half_done else early_tiles)
 
         for v in range(-1, STEPS):
-            if v >= 0 and v in z_paired:
-                prepare(first_matmul(z_paired[v], (0, 1)), z_paired[v], (0, 1))
+            if v in paired_z:
+                prepare(first_matmul(paired_z[v], (0, 1)), paired_z[v], (0, 1))
             if v in to_prepare:
                 prepare(*to_prepare[v])
             for name, g, raw, codes_all, scales_all in turns.get(v, ()):
@@ -278,27 +280,23 @@ def tile_sgcn_pa_kernel(tc, x, rinc, linc, edge_w, out):
                 quantise(grouped[name, g], codes_all[:, g, :], scales_all[:, g, :])
             if 1 <= v < STEPS - 1:
                 quantise_messages(*ORDER[v - 1])
-            due = list(range(v - 1)) if v == y_from else [v - 2] if v > y_from else []
-            for w in due[:1]:
-                sums(w)
-            if v in z_single and v <= last_early:
-                g, h = z_single[v]
+            ready = list(range(v - 1)) if v == sums_from else [v - 2] if v > sums_from else []
+            for made in ready[:1]:
+                sums(made)
+            if v in single_z:
+                g, h = single_z[v]
                 to_prepare[v + 1] = (first_matmul(g, (h,)), g, (h,))
-            for w in due[1:]:
-                sums(w)
-            if v == last_early:
+            for made in ready[1:]:
+                sums(made)
+            if v == first_half_done:
                 store_half(0, all_tiles)
-            late = [ORDER[w] for w in range(v - 1) if ORDER[w][1] == 1] if v == last_early + 1 else []
-            for g, h in late[:2]:
-                second_matmul(g, h, late_tiles)
-            if v > last_early and v in z_single:
-                g, h = z_single[v]
-                to_prepare[v + 1] = (first_matmul(g, (h,)), g, (h,))
-            for g, h in late[2:]:
-                second_matmul(g, h, late_tiles)
+            if v == first_half_done + 1:
+                for g, h in ORDER[:first_half_done]:
+                    if h == 1:
+                        second_matmul(g, h, late_tiles)
             if v == -1:
                 prepare(first_matmul(0, (0, 1)), 0, (0, 1))
         quantise_messages(*ORDER[STEPS - 1])
-        for w in range(STEPS - 2, STEPS):
-            sums(w)
+        for made in range(STEPS - 2, STEPS):
+            sums(made)
         store_half(1, all_tiles)

from contextlib import ExitStack

import concourse.mybir as mybir
from concourse.masks import make_identity

F32 = mybir.dt.float32
BF16 = mybir.dt.bfloat16
U32 = mybir.dt.uint32
U8 = mybir.dt.uint8
FP8X4 = mybir.dt.float8_e4m3fn_x4

P = 128
PACK = 4
K_PASS = P * PACK

SIGNALS, NODES, EDGES, CHANNELS, KERNELS = 8, 512, 4096, 16, 8
PASSES = EDGES // K_PASS
NODE_TILES = NODES // P
HALVES = 2
Z_COLS = SIGNALS * CHANNELS // HALVES
M_COLS = Z_COLS * KERNELS
WORDS = P
SCALAR_FROM = 2
SCALAR_KERNELS = (3, 2)
GPSIMD_COLS = 16
VECTOR_COLS = Z_COLS - GPSIMD_COLS
RUN = 4
BANKS = 6
TURNED_A_STEP = 4
QUANTISED_A_STEP = 3
TURNED_BUFS = 8

FLOPS = 2 * SIGNALS * EDGES * NODES * CHANNELS + 2 * SIGNALS * NODES * EDGES * CHANNELS * KERNELS

SPLIT = 4
PAIRED = PASSES - SPLIT
ORDER = [(g, h) for g in range(PAIRED) for h in range(HALVES)] + [
    (g, h) for h in range(HALVES) for g in range(PAIRED, PASSES)
]
STEPS = len(ORDER)


def scalar_kernels(g, h):
    return SCALAR_KERNELS[h] if g >= SCALAR_FROM else 0


def tile_sgcn_pa_kernel(tc, x, rinc, linc, edge_w, out):
    nc = tc.nc
    with ExitStack() as stack:
        keep = stack.enter_context(tc.tile_pool(name="keep", bufs=1))
        stage = stack.enter_context(tc.tile_pool(name="stage", bufs=3))
        codes = stack.enter_context(tc.tile_pool(name="codes", bufs=1))
        results = stack.enter_context(tc.tile_pool(name="results", bufs=2 * NODE_TILES))
        banks = stack.enter_context(tc.psum_pool(name="banks", bufs=1))
        z_banks = stack.enter_context(tc.psum_pool(name="z_banks", bufs=2))
        stack.enter_context(tc.manual_schedule())

        x_raw = keep.tile([P, SIGNALS, PACK, CHANNELS], BF16)
        w_raw = keep.tile([P, PASSES * PACK * KERNELS], BF16)
        rinc_raw = []
        for g in range(PASSES):
            rows = keep.tile([P, PACK, NODES], BF16, name="rinc_raw%d" % g)
            source = rinc[K_PASS * g : K_PASS * (g + 1), :].rearrange("(p t) n -> p t n", t=PACK)
            pieces = 2 if g == 0 else 1
            for piece in range(pieces):
                part = slice(PACK // pieces * piece, PACK // pieces * (piece + 1))
                nc.sync.dma_start(out=rows[:, part, :], in_=source[:, part, :])
            rinc_raw.append(rows[:].rearrange("p t n -> p (t n)"))
            if g == 1:
                nc.sync.dma_start(
                    out=x_raw[:].rearrange("q b s c -> q b (s c)"),
                    in_=x.rearrange("b (q s) c -> q b (s c)", s=PACK),
                )
            if g == 2:
                nc.sync.dma_start(
                    out=w_raw[:].rearrange("p (g tk) -> p g tk", g=PASSES),
                    in_=edge_w.rearrange("(g p t) k -> p g (t k)", p=P, t=PACK),
                )
        linc_raw = []
        for g in range(PASSES):
            cols = keep.tile([P, NODE_TILES * K_PASS], BF16, name="linc_raw%d" % g)
            nc.sync.dma_start(
                out=cols[:].rearrange("p (i e) -> p i e", i=NODE_TILES),
                in_=linc[:, K_PASS * g : K_PASS * (g + 1)].rearrange("(i p) e -> p i e", p=P),
            )
            linc_raw.append(cols[:])

        ident = keep.tile([P, P], F32)
        make_identity(nc, ident[:])

        w_grouped = keep.tile([P, PASSES, KERNELS, PACK], F32)
        nc.gpsimd.tensor_copy(
            out=w_grouped[:],
            in_=w_raw[:].rearrange("p (g t k) -> p g k t", g=PASSES, k=KERNELS),
        )

        x_codes = keep.tile([P, SIGNALS * CHANNELS], U32, align_bytes=64)
        x_scales = keep.tile([P, SIGNALS * CHANNELS], U8, align_bytes=64)
        rinc_codes = keep.tile([P, PASSES, K_PASS], U32, align_bytes=64)
        rinc_scales = keep.tile([P, PASSES, K_PASS], U8, align_bytes=64)
        linc_codes = keep.tile([P, PASSES, NODES], U32, align_bytes=64)
        linc_scales = keep.tile([P, PASSES, NODES], U8, align_bytes=64)

        x_grouped = keep.tile([P, SIGNALS * CHANNELS * PACK], BF16, align_bytes=64)
        nc.vector.tensor_copy(
            out=x_grouped[:].rearrange("q (b c s) -> q b c s", b=SIGNALS, s=PACK),
            in_=x_raw[:].rearrange("q b s c -> q b c s"),
        )
        nc.vector.quantize_mx(out=x_codes[:].bitcast(FP8X4), scales=x_scales[:], in_=x_grouped[:])

        grouped = {}
        z = {}
        z_gpsimd = {}
        products = {}
        m_codes = {}
        m_scales = {}
        y_acc = {}
        banks_used = []

        def next_bank(shape):
            place = len(banks_used) % BANKS
            bank = banks.tile(shape, F32, name="bank%d" % place)
            banks_used.append(place)
            return bank

        def turn(name, g, raw):
            raw_words = raw.bitcast(F32).rearrange("p (a w) -> p a w", a=4)
            tile = stage.tile([P, PACK * K_PASS], BF16, name="turned", bufs=TURNED_BUFS, align_bytes=64)
            tile_words = tile[:].bitcast(F32).rearrange("p (a r u) -> p a r u", a=4, u=2)
            for pair in range(2):
                bank = next_bank([P, 2, 2, WORDS])
                for a in range(2):
                    for u in range(2):
                        nc.tensor.transpose(bank[:, a, u, :], raw_words[:, 2 * pair + a, u : 2 * WORDS : 2], ident[:])
                nc.scalar.copy(
                    out=tile_words[:, 2 * pair : 2 * pair + 2],
                    in_=bank[:].rearrange("p a u r -> p a r u"),
                )
            grouped[name, g] = tile

        def quantise(tile, codes_ap, scales_ap):
            nc.vector.quantize_mx(out=codes_ap.bitcast(FP8X4), scales=scales_ap, in_=tile[:])

        def first_matmul(g, halves):
            cols = slice(Z_COLS * halves[0], Z_COLS * (halves[-1] + 1))
            tile = z_banks.tile([P, PACK, Z_COLS * len(halves)], F32, name="z")
            for t in range(PACK):
                rows = slice(P * t, P * (t + 1))
                nc.tensor.matmul_mx(
                    out=tile[:, t, :],
                    lhsT=rinc_codes[:, g, rows].bitcast(FP8X4),
                    lhsT_scale=rinc_scales[:, g, rows],
                    rhs=x_codes[:, cols].bitcast(FP8X4),
                    rhs_scale=x_scales[:, cols],
                    start=True,
                    stop=True,
                )
            for place, h in enumerate(halves):
                z[g, h] = tile[:, :, Z_COLS * place : Z_COLS * (place + 1)]
            return tile

        def prepare(tile, g, halves):
            for_gpsimd = stage.tile([P, len(halves), GPSIMD_COLS, PACK], F32, name="z_gpsimd")
            nc.scalar.copy(
                out=for_gpsimd[:],
                in_=tile[:].rearrange("p t (h c) -> p h c t", c=Z_COLS)[:, :, VECTOR_COLS:, :],
            )
            for place, h in enumerate(halves):
                z_gpsimd[g, h] = for_gpsimd[:, place]
            mine = [scalar_kernels(g, h) for h in halves]
            most = max(mine)
            if most == 0:
                return
            runs = stage.tile([P, PACK, len(halves), most, Z_COLS], BF16, name="products")
            for k in range(most):
                count = len([1 for number in mine if k >= most - number])
                for t in range(PACK):
                    nc.scalar.activation(
                        out=runs[:, t, :count, k, :],
                        in_=tile[:, t, : count * Z_COLS].rearrange("p (h c) -> p h c", h=count),
                        func=mybir.ActivationFunctionType.Copy,
                        scale=w_grouped[:, g, KERNELS - most + k, t : t + 1],
                    )
            for place, h in enumerate(halves):
                products[g, h] = runs[:, :, place, most - mine[place] :, :]

        def messages(g, h):
            tile = stage.tile([P, M_COLS * PACK], BF16, name="m_grouped", align_bytes=64)
            planes = tile[:].rearrange("p (k c t) -> p k c t", k=KERNELS, t=PACK)
            others = KERNELS - scalar_kernels(g, h)
            weights = w_grouped[:, g, :others, :].unsqueeze(2)
            shape = [P, others, VECTOR_COLS, PACK]
            nc.vector.tensor_tensor(
                out=planes[:, :others, :VECTOR_COLS, :],
                in0=z[g, h][:, :, :VECTOR_COLS].rearrange("p t c -> p c t").unsqueeze(1).to_broadcast(shape),
                in1=weights.to_broadcast(shape),
                op=mybir.AluOpType.mult,
            )
            shape = [P, others, GPSIMD_COLS, PACK]
            nc.gpsimd.tensor_tensor(
                out=planes[:, :others, VECTOR_COLS:, :],
                in0=z_gpsimd[g, h].unsqueeze(1).to_broadcast(shape),
                in1=weights.to_broadcast(shape),
                op=mybir.AluOpType.mult,
            )
            if others < KERNELS:
                nc.scalar.copy(
                    out=tile[:, others * Z_COLS * PACK :].rearrange("p (b i t) -> p b t i", i=RUN, t=PACK),
                    in_=products[g, h].rearrange("p t k c -> p t (k c)").rearrange("p t (b i) -> p b t i", i=RUN),
                )
            grouped["m", g, h] = tile

        def quantise_messages(g, h):
            m_codes[g, h] = codes.tile([P, M_COLS], U32, name="m_codes%d_%d" % (g, h), align_bytes=64)
            m_scales[g, h] = codes.tile([P, M_COLS], U8, name="m_scales%d_%d" % (g, h), align_bytes=64)
            quantise(grouped["m", g, h], m_codes[g, h][:], m_scales[g, h][:])

        def second_matmul(g, h, node_tiles):
            for i in node_tiles:
                if g == 0:
                    y_acc[h, i] = next_bank([P, M_COLS])
                nodes = slice(P * i, P * (i + 1))
                nc.tensor.matmul_mx(
                    out=y_acc[h, i][:],
                    lhsT=linc_codes[:, g, nodes].bitcast(FP8X4),
                    lhsT_scale=linc_scales[:, g, nodes],
                    rhs=m_codes[g, h][:].bitcast(FP8X4),
                    rhs_scale=m_scales[g, h][:],
                    start=(g == 0),
                    stop=(g == PASSES - 1),
                )

        def store_half(h, node_tiles):
            signals = SIGNALS // HALVES
            for i in node_tiles:
                y_sb = results.tile([P, M_COLS], F32)
                copy = nc.scalar.copy if i % 2 == 0 else nc.vector.tensor_copy
                copy(
                    out=y_sb[:].rearrange("p (c s k) -> p s c k", s=2, k=KERNELS // 2),
                    in_=y_acc[h, i][:].rearrange("p (s k c) -> p s c k", s=2, k=KERNELS // 2),
                )
                nc.sync.dma_start(
                    out=out[signals * h : signals * (h + 1), P * i : P * (i + 1), :].rearrange("b p j -> p b j"),
                    in_=y_sb[:].rearrange("p (b j) -> p b j", b=signals),
                )

        all_tiles = range(NODE_TILES)
        early_tiles = range(BANKS - NODE_TILES)
        late_tiles = range(BANKS - NODE_TILES, NODE_TILES)
        to_turn = [("rinc", g, rinc_raw, rinc_codes, rinc_scales) for g in range(PASSES)] + [
            ("linc", g, linc_raw, linc_codes, linc_scales) for g in range(PASSES)
        ]
        turns = {}
        quantises = {}
        for n, what in enumerate(to_turn):
            turns.setdefault((n - 2) // TURNED_A_STEP, []).append(what)
            quantises.setdefault((n - 1) // QUANTISED_A_STEP, []).append(what)
        sums_from = max(turns) + 1
        first_half_done = ORDER.index((PASSES - 1, 0)) + 2
        paired_z = {2 * g - 1: g for g in range(1, PAIRED)}
        single_z = {made - 2: ORDER[made] for made in range(2 * PAIRED, STEPS)}
        to_prepare = {}

        def sums(made):
            g, h = ORDER[made]
            second_matmul(g, h, all_tiles if h == 0 or made >= first_half_done else early_tiles)

        for v in range(-1, STEPS):
            if v in paired_z:
                prepare(first_matmul(paired_z[v], (0, 1)), paired_z[v], (0, 1))
            if v in to_prepare:
                prepare(*to_prepare[v])
            for name, g, raw, codes_all, scales_all in turns.get(v, ()):
                turn(name, g, raw[g])
            if v == STEPS - 1:
                quantise_messages(*ORDER[v - 1])
            if v >= 0:
                messages(*ORDER[v])
            for name, g, raw, codes_all, scales_all in quantises.get(v, ()):
                quantise(grouped[name, g], codes_all[:, g, :], scales_all[:, g, :])
            if 1 <= v < STEPS - 1:
                quantise_messages(*ORDER[v - 1])
            ready = list(range(v - 1)) if v == sums_from else [v - 2] if v > sums_from else []
            for made in ready[:1]:
                sums(made)
            if v in single_z:
                g, h = single_z[v]
                to_prepare[v + 1] = (first_matmul(g, (h,)), g, (h,))
            for made in ready[1:]:
                sums(made)
            if v == first_half_done:
                store_half(0, all_tiles)
            if v == first_half_done + 1:
                for g, h in ORDER[:first_half_done]:
                    if h == 1:
                        second_matmul(g, h, late_tiles)
            if v == -1:
                prepare(first_matmul(0, (0, 1)), 0, (0, 1))
        quantise_messages(*ORDER[STEPS - 1])
        for made in range(STEPS - 2, STEPS):
            sums(made)
        store_half(1, all_tiles)
